import numpy as np
import ml_dtypes


def mxq(x, axis, fmt="e4m3"):
    dtype, down = {"e4m3": (ml_dtypes.float8_e4m3fn, 7), "e5m2": (ml_dtypes.float8_e5m2, 14)}[fmt]
    v = np.moveaxis(np.asarray(x, np.float32).astype(ml_dtypes.bfloat16).astype(np.float64), axis, -1)
    blocks = v.reshape(v.shape[:-1] + (-1, 32))
    amax = np.abs(blocks).max(-1, keepdims=True)
    byte = np.maximum(np.where(amax > 0, np.frexp(amax)[1] - 1 + 127, 0) - down, 1)
    scale = np.exp2(byte - 127.0)
    codes = (blocks / scale).astype(np.float32).astype(dtype).astype(np.float64)
    return np.moveaxis((codes * scale).reshape(v.shape), -1, axis)


WIDE = False


def mx_kscale(k):
    if not WIDE:
        return np.ones(k)
    levels = np.array([10, -10, 5, -5, 0])
    a = np.random.permutation(np.resize(levels, k // 512 * 4)).reshape(k // 512, 4)
    idx = np.arange(k)
    return np.exp2(a[idx // 512, idx % 128 // 32])


BF16 = ml_dtypes.bfloat16


def bf(x):
    return np.asarray(x, np.float32).astype(BF16)


def f64(x):
    return np.asarray(x).astype(np.float64)


E2M1 = np.array([0.0, 0.5, 1.0, 1.5, 2.0, 3.0, 4.0, 6.0, -0.0, -0.5, -1.0, -1.5, -2.0, -3.0, -4.0, -6.0])


def pack_weight(w, fmt):
    k, n = w.shape
    w = f64(bf(w)).reshape(k // 32, 32, n)
    amax = np.abs(w).max(1)
    if fmt == "e4m3":
        byte = np.frexp(amax)[1] - 1 + 127 - 7
    else:
        mant, ex = np.frexp(amax / 6.0)
        byte = np.where(mant > 0.5, ex, ex - 1) + 127
    byte = np.clip(np.where(amax > 0, byte, 1), 1, 254)
    scaled = (w * np.exp2(127.0 - byte)[:, None, :]).reshape(k, n).astype(np.float32)
    by_word = np.ascontiguousarray(scaled.reshape(k // 512, 128, 4, n).transpose(0, 1, 3, 2))
    if fmt == "e4m3":
        words = by_word.astype(ml_dtypes.float8_e4m3fn).view(np.uint8)
    else:
        c = by_word.astype(ml_dtypes.float4_e2m1fn).view(np.uint8) & 0xF
        words = c[..., 0::2] | (c[..., 1::2] << 4)
    return np.ascontiguousarray(words), np.ascontiguousarray(byte.astype(np.uint8).reshape(k // 512, 16, n))


def unpack_weight(words, scales, fmt):
    g, p, n, _ = words.shape
    if fmt == "e4m3":
        vals = np.ascontiguousarray(words).view(ml_dtypes.float8_e4m3fn).astype(np.float64)
    else:
        nib = np.empty((g, p, n, 4), np.uint8)
        nib[..., 0::2] = words & 0xF
        nib[..., 1::2] = words >> 4
        vals = E2M1[nib]
    vals = vals * np.repeat(np.exp2(scales.astype(np.float64) - 127.0), 8, axis=1)[..., None]
    return vals.transpose(0, 1, 3, 2).reshape(g * 512, n)


B, G, DB, DR = 128, 16, 512, 16384
FMT = "e4m3"


def mish(v):
    return v * np.tanh(np.log(1.0 + np.exp(v)))


def setup_inputs():
    s, t = mx_kscale(DR), mx_kscale(DB)
    BB_feature = bf(np.random.standard_normal((B, G, DB)) * t)
    RF_feature = bf(np.random.standard_normal((B, DR)) * s)
    W_bbbb = np.random.standard_normal((DB, DB)) / np.sqrt(DB) / t
    b_bbbb = bf(np.random.standard_normal(DB) * 0.5)
    W_rfbb = np.random.standard_normal((DB, DR)) / np.sqrt(DR) / s
    b_rfbb = bf(np.random.standard_normal(DB) * 0.5)
    W_bbbb_words, W_bbbb_scales = pack_weight(np.ascontiguousarray(W_bbbb.T), FMT)
    W_rfbb_words, W_rfbb_scales = pack_weight(np.ascontiguousarray(W_rfbb.T), FMT)
    return {"BB_feature": BB_feature,
            "RF_feature": RF_feature,
            "W_bbbb_words": W_bbbb_words,
            "W_bbbb_scales": W_bbbb_scales,
            "b_bbbb": b_bbbb,
            "W_rfbb_words": W_rfbb_words,
            "W_rfbb_scales": W_rfbb_scales,
            "b_rfbb": b_rfbb}


def reference(BB_feature, RF_feature, W_bbbb_words, W_bbbb_scales, b_bbbb, W_rfbb_words, W_rfbb_scales, b_rfbb):
    RF_to_BB = mish((mxq(f64(RF_feature), 1, "e4m3") @ unpack_weight(W_rfbb_words, W_rfbb_scales, FMT)) + f64(b_rfbb))
    BB_to_BB = mish((mxq(f64(BB_feature), 2, "e4m3") @ unpack_weight(W_bbbb_words, W_bbbb_scales, FMT)) + f64(b_bbbb))
    return BB_to_BB + RF_to_BB[:, None, :]

@@ -1,0 +1,229 @@
+from contextlib import ExitStack
+
+import concourse.mybir as mybir
+from concourse.masks import make_identity
+
+F32 = mybir.dt.float32
+BF16 = mybir.dt.bfloat16
+I32 = mybir.dt.int32
+U32 = mybir.dt.uint32
+U8 = mybir.dt.uint8
+FP8X4 = mybir.dt.float8_e4m3fn_x4
+ACT = mybir.ActivationFunctionType
+ALU = mybir.AluOpType
+
+P = 128
+N_OUT = 512
+K_PASS = 512
+PAIRS_PASS = K_PASS // 2
+BB_PASSES = 16
+RF_PASSES = 32
+UNIT = 2
+CHUNK = 4
+BB_UNITS = BB_PASSES // UNIT
+UNITS = (BB_PASSES + RF_PASSES) // UNIT
+SHARED = 4
+PLANE_COLS = RF_PASSES // SHARED
+GPSIMD_UNITS = 4
+LN_FLOOR = 2.0 ** -60
+
+FLOPS = 2 * P * K_PASS * N_OUT * (BB_PASSES + RF_PASSES)
+
+
+def tile_gnn_layer_pb_k_kernel(
+    tc,
+    BB_feature,
+    RF_feature,
+    W_bbbb_words,
+    W_bbbb_scales,
+    b_bbbb,
+    W_rfbb_words,
+    W_rfbb_scales,
+    b_rfbb,
+    out,
+):
+    nc = tc.nc
+    with ExitStack() as stack:
+        stack.enter_context(tc.manual_schedule())
+        keep = stack.enter_context(tc.tile_pool(name="keep", bufs=1))
+        stage = stack.enter_context(tc.tile_pool(name="stage", bufs=3))
+        psum_t = stack.enter_context(tc.psum_pool(name="psum_t", bufs=3))
+        psum_z = stack.enter_context(tc.psum_pool(name="psum_z", bufs=4))
+        psum_acc = stack.enter_context(tc.psum_pool(name="psum_acc", bufs=1))
+
+        wbb_plane = keep.tile([P, N_OUT], U8, name="wbb_plane", align_bytes=64)
+        nc.vector.memset(wbb_plane[:].bitcast(I32), 0)
+        wrf_planes = keep.tile([P, PLANE_COLS, N_OUT], U8, name="wrf_planes", align_bytes=64)
+        nc.vector.memset(wrf_planes[:].bitcast(I32), 0)
+        bias_rows = keep.tile([P, 2, N_OUT], BF16, name="bias_rows")
+        nc.vector.memset(bias_rows[:], 0.0)
+        ones = keep.tile([P, P], BF16, name="ones")
+        nc.vector.memset(ones[:], 1.0)
+        ln_floor = keep.tile([P, 1], F32, name="ln_floor")
+        nc.vector.memset(ln_floor[:], LN_FLOOR)
+        steer = keep.tile([P, 2], F32, name="steer")
+        nc.vector.memset(steer[:], 0.0)
+        ident = keep.tile([P, P], F32, name="ident")
+        make_identity(nc, ident[:])
+
+        features = []
+
+        def load_features(c):
+            chunk = keep.tile([P, CHUNK * K_PASS], BF16, name="features%d" % c)
+            if c < BB_PASSES // CHUNK:
+                rows = BB_feature[:, CHUNK * c : CHUNK * (c + 1), :].rearrange("b g k -> b (g k)")
+            else:
+                first = (CHUNK * c - BB_PASSES) * K_PASS
+                rows = RF_feature[:, first : first + CHUNK * K_PASS]
+            nc.sync.dma_start(out=chunk[:], in_=rows)
+            features.append(chunk)
+
+        def packed_words(dram_words):
+            return dram_words.rearrange("g p n t -> p g (n t)").bitcast(I32)
+
+        nc.scalar.dma_start(out=bias_rows[0:1, 0, :], in_=b_bbbb.rearrange("(o n) -> o n", o=1))
+        nc.scalar.dma_start(out=bias_rows[0:1, 1, :], in_=b_rfbb.rearrange("(o n) -> o n", o=1))
+
+        load_features(0)
+        wbb_words = keep.tile([P, 1, N_OUT], U32, name="wbb_words", align_bytes=64)
+        nc.sync.dma_start(out=wbb_words[:].bitcast(I32), in_=packed_words(W_bbbb_words))
+        for quad in range(4):
+            nc.sync.dma_start(
+                out=wbb_plane[32 * quad : 32 * quad + 4, :].bitcast(I32),
+                in_=W_bbbb_scales[0, 4 * quad : 4 * quad + 4, :].bitcast(I32),
+            )
+        for c in range(1, BB_PASSES // CHUNK):
+            load_features(c)
+
+        for share in range(SHARED):
+            for quad in range(4):
+                first = 32 * quad + 4 * share
+                nc.sync.dma_start(
+                    out=wrf_planes[first : first + 4, :, :].bitcast(I32),
+                    in_=W_rfbb_scales[
+                        PLANE_COLS * share : PLANE_COLS * (share + 1), 4 * quad : 4 * quad + 4, :
+                    ]
+                    .rearrange("j r n -> r j n")
+                    .bitcast(I32),
+                )
+
+        wrf_words = []
+        load_features(BB_PASSES // CHUNK)
+        for c in range(RF_PASSES // CHUNK):
+            if c + 1 < RF_PASSES // CHUNK:
+                load_features(BB_PASSES // CHUNK + c + 1)
+            for half in range(CHUNK // UNIT):
+                g = CHUNK * c + UNIT * half
+                words = keep.tile([P, UNIT, N_OUT], U32, name="wrf_words%d" % (g // UNIT), align_bytes=64)
+                nc.sync.dma_start(out=words[:].bitcast(I32), in_=packed_words(W_rfbb_words[g : g + UNIT]))
+                wrf_words.append(words)
+
+        bias_all = []
+        for which in range(2):
+            spread = psum_z.tile([P, N_OUT], F32, name="zbank")
+            nc.tensor.matmul(out=spread[:], lhsT=ones[:], rhs=bias_rows[:, which, :], start=True, stop=True)
+            bias_sb = keep.tile([P, N_OUT], F32, name="bias_all%d" % which)
+            nc.scalar.copy(out=bias_sb[:], in_=spread[:])
+            bias_all.append(bias_sb)
+        bias_bb, bias_rf = bias_all
+
+        z = [keep.tile([P, UNIT, N_OUT], F32, name="z%d" % u) for u in range(BB_UNITS)]
+        act = [keep.tile([P, UNIT, N_OUT], F32, name="act%d" % u) for u in range(BB_UNITS)]
+        acc = psum_acc.tile([P, N_OUT], F32, name="acc")
+        grouped_of = {}
+        operand_of = {}
+        zbanks_of = {}
+
+        def transpose_unit(s):
+            pairs = features[s // 2][:].bitcast(F32)
+            xt = psum_t.tile([P, UNIT, 2, P], F32, name="xt")
+            for a in range(UNIT):
+                first = (s % 2 * UNIT + a) * PAIRS_PASS
+                for u in range(2):
+                    nc.tensor.transpose(
+                        xt[:, a, u, :], pairs[:, first + u : first + PAIRS_PASS : 2], ident[:]
+                    )
+            grouped = stage.tile([P, UNIT, P, 4], BF16, name="grouped", align_bytes=64)
+            nc.vector.tensor_copy(out=grouped[:].bitcast(F32), in_=xt[:].rearrange("p a u b -> p a b u"))
+            grouped_of[s] = grouped
+
+        def quantise_unit(s):
+            codes = stage.tile([P, UNIT * P], U32, name="codes", align_bytes=64)
+            scales = stage.tile([P, UNIT * P], U8, name="scales", align_bytes=64)
+            nc.vector.quantize_mx(
+                out=codes[:].bitcast(FP8X4),
+                scales=scales[:],
+                in_=grouped_of[s][:].rearrange("p a b t -> p (a b t)"),
+            )
+            operand_of[s] = (codes, scales)
+
+        def multiply_unit(s):
+            codes, scales = operand_of[s]
+            zbanks_of[s] = []
+            for a in range(UNIT):
+                rows = slice(P * a, P * (a + 1))
+                if s < BB_UNITS:
+                    zbank = psum_z.tile([P, N_OUT], F32, name="zbank")
+                    nc.tensor.matmul_mx(
+                        out=zbank[:],
+                        lhsT=codes[:, rows].bitcast(FP8X4),
+                        lhsT_scale=scales[:, rows],
+                        rhs=wbb_words[:, 0, :].bitcast(FP8X4),
+                        rhs_scale=wbb_plane[:],
+                        start=True,
+                        stop=True,
+                    )
+                    zbanks_of[s].append(zbank)
+                else:
+                    g = UNIT * (s - BB_UNITS) + a
+                    nc.tensor.matmul_mx(
+                        out=acc[:],
+                        lhsT=codes[:, rows].bitcast(FP8X4),
+                        lhsT_scale=scales[:, rows],
+                        rhs=wrf_words[s - BB_UNITS][:, a, :].bitcast(FP8X4),
+                        rhs_scale=wrf_planes[4 * (g // PLANE_COLS) : P, g % PLANE_COLS, :],
+                        start=(g == 0),
+                        stop=(g == RF_PASSES - 1),
+                    )
+
+        def bias_unit(u):
+            for a in range(UNIT):
+                nc.vector.tensor_tensor(out=z[u][:, a, :], in0=zbanks_of[u][a][:], in1=bias_bb[:], op=ALU.add)
+            nc.scalar.activation(out=act[u][:], in_=z[u][:], func=ACT.Sigmoid, scale=-1.0)
+
+        for s in range(UNITS + 2):
+            if s < UNITS:
+                transpose_unit(s)
+            if 1 <= s <= UNITS:
+                quantise_unit(s - 1)
+                multiply_unit(s - 1)
+            if 2 <= s < BB_UNITS + 2:
+                bias_unit(s - 2)
+
+        for u in range(BB_UNITS):
+            nc.scalar.activation(out=act[u][:], in_=act[u][:], func=ACT.Ln, bias=ln_floor[:, 0:1])
+        nc.scalar.activation(out=steer[:, 1:2], in_=steer[:, 0:1], func=ACT.Sigmoid)
+        for u in range(BB_UNITS):
+            nc.scalar.activation(out=act[u][:], in_=act[u][:], func=ACT.Tanh, scale=-1.0)
+            if u < GPSIMD_UNITS:
+                nc.gpsimd.tensor_tensor(out=z[u][:], in0=z[u][:], in1=act[u][:], op=ALU.mult)
+
+        z_rf = keep.tile([P, N_OUT], F32, name="z_rf")
+        act_rf = keep.tile([P, N_OUT], F32, name="act_rf")
+        rf = keep.tile([P, N_OUT], F32, name="rf")
+        nc.vector.tensor_tensor(out=z_rf[:], in0=acc[:], in1=bias_rf[:], op=ALU.add)
+        nc.scalar.activation(out=act_rf[:], in_=z_rf[:], func=ACT.Sigmoid, scale=-1.0)
+        nc.scalar.activation(out=act_rf[:], in_=act_rf[:], func=ACT.Ln, bias=ln_floor[:, 0:1])
+        nc.scalar.activation(out=act_rf[:], in_=act_rf[:], func=ACT.Tanh, scale=-1.0)
+        for u in range(GPSIMD_UNITS, BB_UNITS):
+            nc.vector.tensor_tensor(out=z[u][:], in0=z[u][:], in1=act[u][:], op=ALU.mult)
+        nc.vector.tensor_tensor(out=rf[:], in0=z_rf[:], in1=act_rf[:], op=ALU.mult)
+
+        for u in range(BB_UNITS):
+            nc.vector.tensor_tensor(
+                out=z[u][:],
+                in0=z[u][:],
+                in1=rf[:].unsqueeze(1).to_broadcast([P, UNIT, N_OUT]),
+                op=ALU.add,
+            )
+            nc.sync.dma_start(out=out[:, UNIT * u : UNIT * (u + 1), :], in_=z[u][:])

@@ -144,7 +144,11 @@ def tile_gnn_layer_pb_k_kernel(
                         xt[:, a, u, :], pairs[:, first + u : first + PAIRS_PASS : 2], ident[:]
                     )
             grouped = stage.tile([P, UNIT, P, 4], BF16, name="grouped", align_bytes=64)
-            nc.vector.tensor_copy(out=grouped[:].bitcast(F32), in_=xt[:].rearrange("p a u b -> p a b u"))
+            side_by_side = xt[:].rearrange("p a u b -> p a b u")
+            if s < BB_UNITS:
+                nc.scalar.copy(out=grouped[:].bitcast(F32), in_=side_by_side)
+            else:
+                nc.vector.tensor_copy(out=grouped[:].bitcast(F32), in_=side_by_side)
             grouped_of[s] = grouped
 
         def quantise_unit(s):
@@ -191,14 +195,15 @@ def tile_gnn_layer_pb_k_kernel(
                 nc.vector.tensor_tensor(out=z[u][:, a, :], in0=zbanks_of[u][a][:], in1=bias_bb[:], op=ALU.add)
             nc.scalar.activation(out=act[u][:], in_=z[u][:], func=ACT.Sigmoid, scale=-1.0)
 
-        for s in range(UNITS + 2):
+        for s in range(UNITS + 3):
             if s < UNITS:
                 transpose_unit(s)
-            if 1 <= s <= UNITS:
+            if 1 <= s < UNITS + 1:
                 quantise_unit(s - 1)
-                multiply_unit(s - 1)
-            if 2 <= s < BB_UNITS + 2:
-                bias_unit(s - 2)
+            if 2 <= s < UNITS + 2:
+                multiply_unit(s - 2)
+            if 3 <= s < BB_UNITS + 3:
+                bias_unit(s - 3)
 
         for u in range(BB_UNITS):
             nc.scalar.activation(out=act[u][:], in_=act[u][:], func=ACT.Ln, bias=ln_floor[:, 0:1])

@@ -24,7 +24,7 @@ BB_UNITS = BB_PASSES // UNIT
 UNITS = (BB_PASSES + RF_PASSES) // UNIT
 SHARED = 4
 PLANE_COLS = RF_PASSES // SHARED
-GPSIMD_UNITS = 4
+GPSIMD_UNITS = 0
 LN_FLOOR = 2.0 ** -60
 
 FLOPS = 2 * P * K_PASS * N_OUT * (BB_PASSES + RF_PASSES)

@@ -24,6 +24,7 @@ BB_UNITS = BB_PASSES // UNIT
 UNITS = (BB_PASSES + RF_PASSES) // UNIT
 SHARED = 4
 PLANE_COLS = RF_PASSES // SHARED
+SCALAR_COPIES = BB_UNITS + 3
 GPSIMD_UNITS = 0
 LN_FLOOR = 2.0 ** -60
 
@@ -51,6 +52,8 @@ def tile_gnn_layer_pb_k_kernel(
         psum_z = stack.enter_context(tc.psum_pool(name="psum_z", bufs=4))
         psum_acc = stack.enter_context(tc.psum_pool(name="psum_acc", bufs=1))
 
+        steer = keep.tile([P, 2], F32, name="steer")
+        nc.vector.memset(steer[:], 0.0)
         wbb_plane = keep.tile([P, N_OUT], U8, name="wbb_plane", align_bytes=64)
         nc.vector.memset(wbb_plane[:].bitcast(I32), 0)
         wrf_planes = keep.tile([P, PLANE_COLS, N_OUT], U8, name="wrf_planes", align_bytes=64)
@@ -61,8 +64,6 @@ def tile_gnn_layer_pb_k_kernel(
         nc.vector.memset(ones[:], 1.0)
         ln_floor = keep.tile([P, 1], F32, name="ln_floor")
         nc.vector.memset(ln_floor[:], LN_FLOOR)
-        steer = keep.tile([P, 2], F32, name="steer")
-        nc.vector.memset(steer[:], 0.0)
         ident = keep.tile([P, P], F32, name="ident")
         make_identity(nc, ident[:])
 
@@ -83,6 +84,7 @@ def tile_gnn_layer_pb_k_kernel(
 
         nc.scalar.dma_start(out=bias_rows[0:1, 0, :], in_=b_bbbb.rearrange("(o n) -> o n", o=1))
         nc.scalar.dma_start(out=bias_rows[0:1, 1, :], in_=b_rfbb.rearrange("(o n) -> o n", o=1))
+        nc.scalar.activation(out=steer[:, 1:2], in_=steer[:, 0:1], func=ACT.Sigmoid)
 
         load_features(0)
         wbb_words = keep.tile([P, 1, N_OUT], U32, name="wbb_words", align_bytes=64)
@@ -123,7 +125,7 @@ def tile_gnn_layer_pb_k_kernel(
             spread = psum_z.tile([P, N_OUT], F32, name="zbank")
             nc.tensor.matmul(out=spread[:], lhsT=ones[:], rhs=bias_rows[:, which, :], start=True, stop=True)
             bias_sb = keep.tile([P, N_OUT], F32, name="bias_all%d" % which)
-            nc.scalar.copy(out=bias_sb[:], in_=spread[:])
+            nc.vector.tensor_copy(out=bias_sb[:], in_=spread[:])
             bias_all.append(bias_sb)
         bias_bb, bias_rf = bias_all
 
@@ -145,7 +147,7 @@ def tile_gnn_layer_pb_k_kernel(
                     )
             grouped = stage.tile([P, UNIT, P, 4], BF16, name="grouped", align_bytes=64)
             side_by_side = xt[:].rearrange("p a u b -> p a b u")
-            if s < BB_UNITS:
+            if s < SCALAR_COPIES:
                 nc.scalar.copy(out=grouped[:].bitcast(F32), in_=side_by_side)
             else:
                 nc.vector.tensor_copy(out=grouped[:].bitcast(F32), in_=side_by_side)

@@ -89,23 +89,20 @@ def tile_gnn_layer_pb_k_kernel(
         load_features(0)
         wbb_words = keep.tile([P, 1, N_OUT], U32, name="wbb_words", align_bytes=64)
         nc.sync.dma_start(out=wbb_words[:].bitcast(I32), in_=packed_words(W_bbbb_words))
-        for quad in range(4):
+        for r in range(4):
             nc.sync.dma_start(
-                out=wbb_plane[32 * quad : 32 * quad + 4, :].bitcast(I32),
-                in_=W_bbbb_scales[0, 4 * quad : 4 * quad + 4, :].bitcast(I32),
+                out=wbb_plane[r : P : 32, :].bitcast(I32),
+                in_=W_bbbb_scales[0, r : 16 : 4, :].bitcast(I32),
             )
         for c in range(1, BB_PASSES // CHUNK):
             load_features(c)
 
         for share in range(SHARED):
-            for quad in range(4):
-                first = 32 * quad + 4 * share
+            for r in range(4):
                 nc.sync.dma_start(
-                    out=wrf_planes[first : first + 4, :, :].bitcast(I32),
-                    in_=W_rfbb_scales[
-                        PLANE_COLS * share : PLANE_COLS * (share + 1), 4 * quad : 4 * quad + 4, :
-                    ]
-                    .rearrange("j r n -> r j n")
+                    out=wrf_planes[4 * share + r : P : 32, :, :].bitcast(I32),
+                    in_=W_rfbb_scales[PLANE_COLS * share : PLANE_COLS * (share + 1), r : 16 : 4, :]
+                    .rearrange("j q n -> q j n")
                     .bitcast(I32),
                 )
 

@@ -25,7 +25,7 @@ UNITS = (BB_PASSES + RF_PASSES) // UNIT
 SHARED = 4
 PLANE_COLS = RF_PASSES // SHARED
 SCALAR_COPIES = BB_UNITS + 3
-GPSIMD_UNITS = 0
+EARLY_PRODUCTS = 3
 LN_FLOOR = 2.0 ** -60
 
 FLOPS = 2 * P * K_PASS * N_OUT * (BB_PASSES + RF_PASSES)
@@ -209,8 +209,9 @@ def tile_gnn_layer_pb_k_kernel(
         nc.scalar.activation(out=steer[:, 1:2], in_=steer[:, 0:1], func=ACT.Sigmoid)
         for u in range(BB_UNITS):
             nc.scalar.activation(out=act[u][:], in_=act[u][:], func=ACT.Tanh, scale=-1.0)
-            if u < GPSIMD_UNITS:
-                nc.gpsimd.tensor_tensor(out=z[u][:], in0=z[u][:], in1=act[u][:], op=ALU.mult)
+
+        for u in range(EARLY_PRODUCTS):
+            nc.vector.tensor_tensor(out=z[u][:], in0=z[u][:], in1=act[u][:], op=ALU.mult)
 
         z_rf = keep.tile([P, N_OUT], F32, name="z_rf")
         act_rf = keep.tile([P, N_OUT], F32, name="act_rf")
@@ -219,7 +220,7 @@ def tile_gnn_layer_pb_k_kernel(
         nc.scalar.activation(out=act_rf[:], in_=z_rf[:], func=ACT.Sigmoid, scale=-1.0)
         nc.scalar.activation(out=act_rf[:], in_=act_rf[:], func=ACT.Ln, bias=ln_floor[:, 0:1])
         nc.scalar.activation(out=act_rf[:], in_=act_rf[:], func=ACT.Tanh, scale=-1.0)
-        for u in range(GPSIMD_UNITS, BB_UNITS):
+        for u in range(EARLY_PRODUCTS, BB_UNITS):
             nc.vector.tensor_tensor(out=z[u][:], in0=z[u][:], in1=act[u][:], op=ALU.mult)
         nc.vector.tensor_tensor(out=rf[:], in0=z_rf[:], in1=act_rf[:], op=ALU.mult)
 

@@ -19,11 +19,11 @@ PAIRS_PASS = K_PASS // 2
 BB_PASSES = 16
 RF_PASSES = 32
 UNIT = 2
-CHUNK = 4
 BB_UNITS = BB_PASSES // UNIT
 UNITS = (BB_PASSES + RF_PASSES) // UNIT
-SHARED = 4
-PLANE_COLS = RF_PASSES // SHARED
+PLANE_COLS = 8
+RF_LOAD = 4
+RF_AHEAD = 2
 SCALAR_COPIES = BB_UNITS + 3
 EARLY_PRODUCTS = 3
 LN_FLOOR = 2.0 ** -60
@@ -56,8 +56,11 @@ def tile_gnn_layer_pb_k_kernel(
         nc.vector.memset(steer[:], 0.0)
         wbb_plane = keep.tile([P, N_OUT], U8, name="wbb_plane", align_bytes=64)
         nc.vector.memset(wbb_plane[:].bitcast(I32), 0)
-        wrf_planes = keep.tile([P, PLANE_COLS, N_OUT], U8, name="wrf_planes", align_bytes=64)
-        nc.vector.memset(wrf_planes[:].bitcast(I32), 0)
+        wrf_planes = []
+        for half in range(2):
+            planes = keep.tile([P, PLANE_COLS, N_OUT], U8, name="wrf_planes%d" % half, align_bytes=64)
+            nc.vector.memset(planes[:].bitcast(I32), 0)
+            wrf_planes.append(planes)
         bias_rows = keep.tile([P, 2, N_OUT], BF16, name="bias_rows")
         nc.vector.memset(bias_rows[:], 0.0)
         ones = keep.tile([P, P], BF16, name="ones")
@@ -67,26 +70,51 @@ def tile_gnn_layer_pb_k_kernel(
         ident = keep.tile([P, P], F32, name="ident")
         make_identity(nc, ident[:])
 
-        features = []
+        features_of = {}
 
-        def load_features(c):
-            chunk = keep.tile([P, CHUNK * K_PASS], BF16, name="features%d" % c)
-            if c < BB_PASSES // CHUNK:
-                rows = BB_feature[:, CHUNK * c : CHUNK * (c + 1), :].rearrange("b g k -> b (g k)")
+        def load_features(first_unit, units):
+            passes = UNIT * units
+            rows_sb = keep.tile([P, passes * K_PASS], BF16, name="features%d" % first_unit)
+            if first_unit < BB_UNITS:
+                g = UNIT * first_unit
+                rows = BB_feature[:, g : g + passes, :].rearrange("b g k -> b (g k)")
             else:
-                first = (CHUNK * c - BB_PASSES) * K_PASS
-                rows = RF_feature[:, first : first + CHUNK * K_PASS]
-            nc.sync.dma_start(out=chunk[:], in_=rows)
-            features.append(chunk)
+                first = UNIT * (first_unit - BB_UNITS) * K_PASS
+                rows = RF_feature[:, first : first + passes * K_PASS]
+            nc.sync.dma_start(out=rows_sb[:], in_=rows)
+            for j in range(units):
+                features_of[first_unit + j] = (rows_sb, UNIT * j)
 
         def packed_words(dram_words):
             return dram_words.rearrange("g p n t -> p g (n t)").bitcast(I32)
+
+        wrf_words = {}
+
+        def load_words(s):
+            g = UNIT * (s - BB_UNITS)
+            words = keep.tile([P, UNIT, N_OUT], U32, name="wrf_words%d" % s, align_bytes=64)
+            nc.sync.dma_start(out=words[:].bitcast(I32), in_=packed_words(W_rfbb_words[g : g + UNIT]))
+            wrf_words[s] = words
+
+        scale_loads = [(half, share, r) for half in range(2) for share in range(2) for r in range(4)]
+
+        def load_scales(count):
+            for load in scale_loads[:count]:
+                half, share, r = load
+                first = 2 * PLANE_COLS * half + PLANE_COLS * share
+                nc.sync.dma_start(
+                    out=wrf_planes[half][4 * share + r : P : 32, :, :].bitcast(I32),
+                    in_=W_rfbb_scales[first : first + PLANE_COLS, r : 16 : 4, :]
+                    .rearrange("j q n -> q j n")
+                    .bitcast(I32),
+                )
+                scale_loads.remove(load)
 
         nc.scalar.dma_start(out=bias_rows[0:1, 0, :], in_=b_bbbb.rearrange("(o n) -> o n", o=1))
         nc.scalar.dma_start(out=bias_rows[0:1, 1, :], in_=b_rfbb.rearrange("(o n) -> o n", o=1))
         nc.scalar.activation(out=steer[:, 1:2], in_=steer[:, 0:1], func=ACT.Sigmoid)
 
-        load_features(0)
+        load_features(0, 1)
         wbb_words = keep.tile([P, 1, N_OUT], U32, name="wbb_words", align_bytes=64)
         nc.sync.dma_start(out=wbb_words[:].bitcast(I32), in_=packed_words(W_bbbb_words))
         for r in range(4):
@@ -94,28 +122,19 @@ def tile_gnn_layer_pb_k_kernel(
                 out=wbb_plane[r : P : 32, :].bitcast(I32),
                 in_=W_bbbb_scales[0, r : 16 : 4, :].bitcast(I32),
             )
-        for c in range(1, BB_PASSES // CHUNK):
-            load_features(c)
+        load_features(1, 1)
+        for first_unit in range(2, BB_UNITS, 2):
+            load_features(first_unit, 2)
 
-        for share in range(SHARED):
-            for r in range(4):
-                nc.sync.dma_start(
-                    out=wrf_planes[4 * share + r : P : 32, :, :].bitcast(I32),
-                    in_=W_rfbb_scales[PLANE_COLS * share : PLANE_COLS * (share + 1), r : 16 : 4, :]
-                    .rearrange("j q n -> q j n")
-                    .bitcast(I32),
-                )
-
-        wrf_words = []
-        load_features(BB_PASSES // CHUNK)
-        for c in range(RF_PASSES // CHUNK):
-            if c + 1 < RF_PASSES // CHUNK:
-                load_features(BB_PASSES // CHUNK + c + 1)
-            for half in range(CHUNK // UNIT):
-                g = CHUNK * c + UNIT * half
-                words = keep.tile([P, UNIT, N_OUT], U32, name="wrf_words%d" % (g // UNIT), align_bytes=64)
-                nc.sync.dma_start(out=words[:].bitcast(I32), in_=packed_words(W_rfbb_words[g : g + UNIT]))
-                wrf_words.append(words)
+        for s in range(BB_UNITS, UNITS):
+            if s == BB_UNITS:
+                load_features(s, RF_LOAD)
+                load_scales(2)
+            if (s - BB_UNITS) % RF_LOAD == RF_LOAD - RF_AHEAD and s + RF_AHEAD < UNITS:
+                load_features(s + RF_AHEAD, RF_LOAD)
+                load_scales(2)
+            load_words(s)
+            load_scales(2)
 
         bias_all = []
         for which in range(2):
@@ -134,10 +153,11 @@ def tile_gnn_layer_pb_k_kernel(
         zbanks_of = {}
 
         def transpose_unit(s):
-            pairs = features[s // 2][:].bitcast(F32)
+            rows_sb, first_pass = features_of[s]
+            pairs = rows_sb[:].bitcast(F32)
             xt = psum_t.tile([P, UNIT, 2, P], F32, name="xt")
             for a in range(UNIT):
-                first = (s % 2 * UNIT + a) * PAIRS_PASS
+                first = (first_pass + a) * PAIRS_PASS
                 for u in range(2):
                     nc.tensor.transpose(
                         xt[:, a, u, :], pairs[:, first + u : first + PAIRS_PASS : 2], ident[:]
@@ -183,8 +203,10 @@ def tile_gnn_layer_pb_k_kernel(
                         out=acc[:],
                         lhsT=codes[:, rows].bitcast(FP8X4),
                         lhsT_scale=scales[:, rows],
-                        rhs=wrf_words[s - BB_UNITS][:, a, :].bitcast(FP8X4),
-                        rhs_scale=wrf_planes[4 * (g // PLANE_COLS) : P, g % PLANE_COLS, :],
+                        rhs=wrf_words[s][:, a, :].bitcast(FP8X4),
+                        rhs_scale=wrf_planes[g // (2 * PLANE_COLS)][
+                            4 * (g // PLANE_COLS % 2) : P, g % PLANE_COLS, :
+                        ],
                         start=(g == 0),
                         stop=(g == RF_PASSES - 1),
                     )

@@ -14,6 +14,7 @@ ALU = mybir.AluOpType
 
 P = 128
 N_OUT = 512
+N_TILES = N_OUT // P
 K_PASS = 512
 PAIRS_PASS = K_PASS // 2
 BB_PASSES = 16
@@ -21,11 +22,16 @@ RF_PASSES = 32
 UNIT = 2
 BB_UNITS = BB_PASSES // UNIT
 UNITS = (BB_PASSES + RF_PASSES) // UNIT
+CHUNK = 4
+BB_CHUNKS = BB_PASSES // CHUNK
 PLANE_COLS = 8
 RF_LOAD = 4
 RF_AHEAD = 2
-SCALAR_COPIES = BB_UNITS + 3
-EARLY_PRODUCTS = 3
+HALF = N_OUT // 2
+LATE = BB_UNITS + 8
+LATE_LOAD = 2
+FIRST_PRODUCT = BB_UNITS + 11
+STAGED = 4
 LN_FLOOR = 2.0 ** -60
 
 FLOPS = 2 * P * K_PASS * N_OUT * (BB_PASSES + RF_PASSES)
@@ -48,10 +54,15 @@ def tile_gnn_layer_pb_k_kernel(
         stack.enter_context(tc.manual_schedule())
         keep = stack.enter_context(tc.tile_pool(name="keep", bufs=1))
         stage = stack.enter_context(tc.tile_pool(name="stage", bufs=3))
-        psum_t = stack.enter_context(tc.psum_pool(name="psum_t", bufs=3))
-        psum_z = stack.enter_context(tc.psum_pool(name="psum_z", bufs=4))
+        stage_bb = stack.enter_context(tc.tile_pool(name="stage_bb", bufs=2))
+        outs = stack.enter_context(tc.tile_pool(name="outs", bufs=4))
+        psum = stack.enter_context(tc.psum_pool(name="psum", bufs=7))
         psum_acc = stack.enter_context(tc.psum_pool(name="psum_acc", bufs=1))
 
+        bias_tiles = keep.tile([P, P], BF16, name="bias_tiles")
+        nc.vector.memset(bias_tiles[:], 0.0)
+        bias_row = keep.tile([P, N_OUT], BF16, name="bias_row")
+        nc.vector.memset(bias_row[:], 0.0)
         steer = keep.tile([P, 2], F32, name="steer")
         nc.vector.memset(steer[:], 0.0)
         wbb_plane = keep.tile([P, N_OUT], U8, name="wbb_plane", align_bytes=64)
@@ -61,14 +72,14 @@ def tile_gnn_layer_pb_k_kernel(
             planes = keep.tile([P, PLANE_COLS, N_OUT], U8, name="wrf_planes%d" % half, align_bytes=64)
             nc.vector.memset(planes[:].bitcast(I32), 0)
             wrf_planes.append(planes)
-        bias_rows = keep.tile([P, 2, N_OUT], BF16, name="bias_rows")
-        nc.vector.memset(bias_rows[:], 0.0)
         ones = keep.tile([P, P], BF16, name="ones")
         nc.vector.memset(ones[:], 1.0)
         ln_floor = keep.tile([P, 1], F32, name="ln_floor")
         nc.vector.memset(ln_floor[:], LN_FLOOR)
         ident = keep.tile([P, P], F32, name="ident")
         make_identity(nc, ident[:])
+        ident_bf = keep.tile([P, P], BF16, name="ident_bf")
+        make_identity(nc, ident_bf[:])
 
         features_of = {}
 
@@ -96,6 +107,19 @@ def tile_gnn_layer_pb_k_kernel(
             nc.sync.dma_start(out=words[:].bitcast(I32), in_=packed_words(W_rfbb_words[g : g + UNIT]))
             wrf_words[s] = words
 
+        half_words = {}
+
+        def load_half_words(s, h):
+            g = UNIT * (s - BB_UNITS)
+            passes = UNIT * LATE_LOAD
+            words = keep.tile([P, passes, HALF], U32, name="half_words%d_%d" % (s, h), align_bytes=64)
+            nc.sync.dma_start(
+                out=words[:].bitcast(I32),
+                in_=packed_words(W_rfbb_words[g : g + passes, :, HALF * h : HALF * (h + 1), :]),
+            )
+            for j in range(LATE_LOAD):
+                half_words[(s + j, h)] = (words, UNIT * j)
+
         scale_loads = [(half, share, r) for half in range(2) for share in range(2) for r in range(4)]
 
         def load_scales(count):
@@ -110,8 +134,8 @@ def tile_gnn_layer_pb_k_kernel(
                 )
                 scale_loads.remove(load)
 
-        nc.scalar.dma_start(out=bias_rows[0:1, 0, :], in_=b_bbbb.rearrange("(o n) -> o n", o=1))
-        nc.scalar.dma_start(out=bias_rows[0:1, 1, :], in_=b_rfbb.rearrange("(o n) -> o n", o=1))
+        nc.scalar.dma_start(out=bias_tiles[0:N_TILES, :], in_=b_bbbb.rearrange("(i m) -> i m", i=N_TILES))
+        nc.scalar.dma_start(out=bias_row[0:1, :], in_=b_rfbb.rearrange("(o n) -> o n", o=1))
         nc.scalar.activation(out=steer[:, 1:2], in_=steer[:, 0:1], func=ACT.Sigmoid)
 
         load_features(0, 1)
@@ -133,124 +157,221 @@ def tile_gnn_layer_pb_k_kernel(
             if (s - BB_UNITS) % RF_LOAD == RF_LOAD - RF_AHEAD and s + RF_AHEAD < UNITS:
                 load_features(s + RF_AHEAD, RF_LOAD)
                 load_scales(2)
-            load_words(s)
+            if s < LATE:
+                load_words(s)
+            elif (s - LATE) % LATE_LOAD == 0:
+                load_half_words(s, 0)
             load_scales(2)
+        for s in range(LATE, UNITS, LATE_LOAD):
+            load_half_words(s, 1)
 
-        bias_all = []
-        for which in range(2):
-            spread = psum_z.tile([P, N_OUT], F32, name="zbank")
-            nc.tensor.matmul(out=spread[:], lhsT=ones[:], rhs=bias_rows[:, which, :], start=True, stop=True)
-            bias_sb = keep.tile([P, N_OUT], F32, name="bias_all%d" % which)
-            nc.vector.tensor_copy(out=bias_sb[:], in_=spread[:])
-            bias_all.append(bias_sb)
-        bias_bb, bias_rf = bias_all
-
-        z = [keep.tile([P, UNIT, N_OUT], F32, name="z%d" % u) for u in range(BB_UNITS)]
-        act = [keep.tile([P, UNIT, N_OUT], F32, name="act%d" % u) for u in range(BB_UNITS)]
-        acc = psum_acc.tile([P, N_OUT], F32, name="acc")
-        grouped_of = {}
-        operand_of = {}
-        zbanks_of = {}
+        columns = psum.tile([P, N_OUT], F32, name="bank")
+        nc.tensor.matmul(
+            out=columns[:, 0:N_TILES], lhsT=bias_tiles[:], rhs=ident_bf[:, 0:N_TILES], start=True, stop=True
+        )
+        bias_bb = keep.tile([P, N_TILES], F32, name="bias_bb")
+        nc.vector.tensor_copy(out=bias_bb[:], in_=columns[:, 0:N_TILES])
+        minus_bias_bb = keep.tile([P, N_TILES], F32, name="minus_bias_bb")
+        nc.vector.tensor_scalar_mul(out=minus_bias_bb[:], in0=columns[:, 0:N_TILES], scalar1=-1.0)
+        spread = psum.tile([P, N_OUT], F32, name="bank")
+        nc.tensor.matmul(out=spread[:], lhsT=ones[:], rhs=bias_row[:], start=True, stop=True)
+        bias_rf = keep.tile([P, N_OUT], F32, name="bias_rf")
+        nc.vector.tensor_copy(out=bias_rf[:], in_=spread[:])
 
         def transpose_unit(s):
             rows_sb, first_pass = features_of[s]
             pairs = rows_sb[:].bitcast(F32)
-            xt = psum_t.tile([P, UNIT, 2, P], F32, name="xt")
+            xt = psum.tile([P, UNIT, 2, P], F32, name="bank")
             for a in range(UNIT):
                 first = (first_pass + a) * PAIRS_PASS
                 for u in range(2):
                     nc.tensor.transpose(
                         xt[:, a, u, :], pairs[:, first + u : first + PAIRS_PASS : 2], ident[:]
                     )
+            return xt
+
+        def copy_unit(xt, words):
+            nc.vector.tensor_copy(out=words, in_=xt[:].rearrange("p a u b -> p a b u"))
+
+        def quantise(grouped, codes, scales):
+            nc.vector.quantize_mx(
+                out=codes[:].bitcast(FP8X4), scales=scales[:], in_=grouped[:].rearrange("p a b t -> p (a b t)")
+            )
+
+        bb_codes = [keep.tile([P, CHUNK * P], U32, name="bb_codes%d" % c, align_bytes=64) for c in range(BB_CHUNKS)]
+        bb_scales = [keep.tile([P, CHUNK * P], U8, name="bb_scales%d" % c, align_bytes=64) for c in range(BB_CHUNKS)]
+        act = [keep.tile([P, N_TILES, N_OUT], F32, name="act%d" % c) for c in range(BB_CHUNKS)]
+
+        def bb_product(c, i):
+            features_i = slice(P * i, P * (i + 1))
+            zt = psum.tile([P, N_OUT], F32, name="bank")
+            nc.tensor.matmul_mx(
+                out=zt[:],
+                lhsT=wbb_words[:, 0, features_i].bitcast(FP8X4),
+                lhsT_scale=wbb_plane[:, features_i],
+                rhs=bb_codes[c][:].bitcast(FP8X4),
+                rhs_scale=bb_scales[c][:],
+                start=True,
+                stop=True,
+            )
+            return zt
+
+        def bb_front(c):
+            banks = [transpose_unit(2 * c + j) for j in range(2)]
+            grouped = stage_bb.tile([P, CHUNK, P, 4], BF16, name="grouped_bb", align_bytes=64)
+            for j in range(2):
+                copy_unit(banks[j], grouped[:, UNIT * j : UNIT * (j + 1), :, :].bitcast(F32))
+            quantise(grouped, bb_codes[c], bb_scales[c])
+
+        def bb_sigmoids(c):
+            for i in range(N_TILES):
+                zt = bb_product(c, i)
+                nc.scalar.activation(
+                    out=act[c][:, i, :], in_=zt[:], func=ACT.Sigmoid, scale=-1.0, bias=minus_bias_bb[:, i : i + 1]
+                )
+
+        bb_front(0)
+        for c in range(BB_CHUNKS):
+            if c + 1 < BB_CHUNKS:
+                bb_front(c + 1)
+            bb_sigmoids(c)
+
+        for c in range(BB_CHUNKS):
+            nc.scalar.activation(out=act[c][:], in_=act[c][:], func=ACT.Ln, bias=ln_floor[:, 0:1])
+        nc.scalar.activation(out=steer[:, 1:2], in_=steer[:, 0:1], func=ACT.Sigmoid)
+        products = []
+        for h in range(2):
+            for c in range(BB_CHUNKS):
+                pair = act[c][:, 2 * h : 2 * h + 2, :]
+                nc.scalar.activation(out=pair, in_=pair, func=ACT.Tanh, scale=-1.0)
+                products.append([(c, 2 * h), (c, 2 * h + 1)])
+
+        def bb_mish(pair):
+            for c, i in pair:
+                zt = bb_product(c, i)
+                nc.vector.scalar_tensor_tensor(
+                    out=act[c][:, i, :],
+                    in0=zt[:],
+                    scalar=bias_bb[:, i : i + 1],
+                    in1=act[c][:, i, :],
+                    op0=ALU.add,
+                    op1=ALU.mult,
+                )
+
+        grouped_of = {}
+        operand_of = {}
+
+        def rf_front(s):
+            xt = transpose_unit(s)
             grouped = stage.tile([P, UNIT, P, 4], BF16, name="grouped", align_bytes=64)
-            side_by_side = xt[:].rearrange("p a u b -> p a b u")
-            if s < SCALAR_COPIES:
-                nc.scalar.copy(out=grouped[:].bitcast(F32), in_=side_by_side)
-            else:
-                nc.vector.tensor_copy(out=grouped[:].bitcast(F32), in_=side_by_side)
+            copy_unit(xt, grouped[:].bitcast(F32))
             grouped_of[s] = grouped
 
-        def quantise_unit(s):
-            codes = stage.tile([P, UNIT * P], U32, name="codes", align_bytes=64)
-            scales = stage.tile([P, UNIT * P], U8, name="scales", align_bytes=64)
-            nc.vector.quantize_mx(
-                out=codes[:].bitcast(FP8X4),
-                scales=scales[:],
-                in_=grouped_of[s][:].rearrange("p a b t -> p (a b t)"),
-            )
+        def rf_quantise(s):
+            if s < LATE:
+                codes = stage.tile([P, UNIT * P], U32, name="codes", align_bytes=64)
+                scales = stage.tile([P, UNIT * P], U8, name="scales", align_bytes=64)
+            else:
+                codes = keep.tile([P, UNIT * P], U32, name="late_codes%d" % s, align_bytes=64)
+                scales = keep.tile([P, UNIT * P], U8, name="late_scales%d" % s, align_bytes=64)
+            quantise(grouped_of[s], codes, scales)
             operand_of[s] = (codes, scales)
 
-        def multiply_unit(s):
+        def rf_multiply(s, sums, columns_h, first, last):
             codes, scales = operand_of[s]
-            zbanks_of[s] = []
             for a in range(UNIT):
                 rows = slice(P * a, P * (a + 1))
-                if s < BB_UNITS:
-                    zbank = psum_z.tile([P, N_OUT], F32, name="zbank")
-                    nc.tensor.matmul_mx(
-                        out=zbank[:],
-                        lhsT=codes[:, rows].bitcast(FP8X4),
-                        lhsT_scale=scales[:, rows],
-                        rhs=wbb_words[:, 0, :].bitcast(FP8X4),
-                        rhs_scale=wbb_plane[:],
-                        start=True,
-                        stop=True,
-                    )
-                    zbanks_of[s].append(zbank)
+                g = UNIT * (s - BB_UNITS) + a
+                plane = wrf_planes[g // (2 * PLANE_COLS)]
+                offset = 4 * (g // PLANE_COLS % 2)
+                if columns_h is None:
+                    target = sums[:]
+                    rhs = wrf_words[s][:, a, :]
+                    rhs_scale = plane[offset:P, g % PLANE_COLS, :]
                 else:
-                    g = UNIT * (s - BB_UNITS) + a
-                    nc.tensor.matmul_mx(
-                        out=acc[:],
-                        lhsT=codes[:, rows].bitcast(FP8X4),
-                        lhsT_scale=scales[:, rows],
-                        rhs=wrf_words[s][:, a, :].bitcast(FP8X4),
-                        rhs_scale=wrf_planes[g // (2 * PLANE_COLS)][
-                            4 * (g // PLANE_COLS % 2) : P, g % PLANE_COLS, :
-                        ],
-                        start=(g == 0),
-                        stop=(g == RF_PASSES - 1),
-                    )
+                    cols = slice(HALF * columns_h, HALF * (columns_h + 1))
+                    words, first_pass = half_words[(s, columns_h)]
+                    target = sums[:, cols]
+                    rhs = words[:, first_pass + a, :]
+                    rhs_scale = plane[offset:P, g % PLANE_COLS, cols]
+                nc.tensor.matmul_mx(
+                    out=target,
+                    lhsT=codes[:, rows].bitcast(FP8X4),
+                    lhsT_scale=scales[:, rows],
+                    rhs=rhs.bitcast(FP8X4),
+                    rhs_scale=rhs_scale,
+                    start=(g == first),
+                    stop=(g == last),
+                )
 
-        def bias_unit(u):
-            for a in range(UNIT):
-                nc.vector.tensor_tensor(out=z[u][:, a, :], in0=zbanks_of[u][a][:], in1=bias_bb[:], op=ALU.add)
-            nc.scalar.activation(out=act[u][:], in_=z[u][:], func=ACT.Sigmoid, scale=-1.0)
-
-        for s in range(UNITS + 3):
+        early_last = UNIT * (LATE - BB_UNITS) - 1
+        z_early = keep.tile([P, N_OUT], F32, name="z_early")
+        sums_of = {}
+        for s in range(BB_UNITS, UNITS + 2):
             if s < UNITS:
-                transpose_unit(s)
-            if 1 <= s < UNITS + 1:
-                quantise_unit(s - 1)
-            if 2 <= s < UNITS + 2:
-                multiply_unit(s - 2)
-            if 3 <= s < BB_UNITS + 3:
-                bias_unit(s - 3)
-
-        for u in range(BB_UNITS):
-            nc.scalar.activation(out=act[u][:], in_=act[u][:], func=ACT.Ln, bias=ln_floor[:, 0:1])
-        nc.scalar.activation(out=steer[:, 1:2], in_=steer[:, 0:1], func=ACT.Sigmoid)
-        for u in range(BB_UNITS):
-            nc.scalar.activation(out=act[u][:], in_=act[u][:], func=ACT.Tanh, scale=-1.0)
-
-        for u in range(EARLY_PRODUCTS):
-            nc.vector.tensor_tensor(out=z[u][:], in0=z[u][:], in1=act[u][:], op=ALU.mult)
+                rf_front(s)
+            if BB_UNITS + 1 <= s < UNITS + 1:
+                rf_quantise(s - 1)
+            if BB_UNITS + 2 <= s:
+                if s - 2 == BB_UNITS or s - 2 == LATE:
+                    sums_of[s - 2 >= LATE] = psum_acc.tile([P, N_OUT], F32, name="acc")
+                if s - 2 < LATE:
+                    rf_multiply(s - 2, sums_of[False], None, 0, early_last)
+                else:
+                    rf_multiply(s - 2, sums_of[True], 0, early_last + 1, RF_PASSES - 1)
+                if s - 2 == LATE - 1:
+                    nc.vector.tensor_tensor(out=z_early[:], in0=sums_of[False][:], in1=bias_rf[:], op=ALU.add)
+            if FIRST_PRODUCT <= s - 2 < FIRST_PRODUCT + BB_CHUNKS:
+                bb_mish(products[s - 2 - FIRST_PRODUCT])
+        late_sums = sums_of[True]
 
         z_rf = keep.tile([P, N_OUT], F32, name="z_rf")
         act_rf = keep.tile([P, N_OUT], F32, name="act_rf")
         rf = keep.tile([P, N_OUT], F32, name="rf")
-        nc.vector.tensor_tensor(out=z_rf[:], in0=acc[:], in1=bias_rf[:], op=ALU.add)
-        nc.scalar.activation(out=act_rf[:], in_=z_rf[:], func=ACT.Sigmoid, scale=-1.0)
-        nc.scalar.activation(out=act_rf[:], in_=act_rf[:], func=ACT.Ln, bias=ln_floor[:, 0:1])
-        nc.scalar.activation(out=act_rf[:], in_=act_rf[:], func=ACT.Tanh, scale=-1.0)
-        for u in range(EARLY_PRODUCTS, BB_UNITS):
-            nc.vector.tensor_tensor(out=z[u][:], in0=z[u][:], in1=act[u][:], op=ALU.mult)
-        nc.vector.tensor_tensor(out=rf[:], in0=z_rf[:], in1=act_rf[:], op=ALU.mult)
 
-        for u in range(BB_UNITS):
+        def rf_mish(h):
+            cols = slice(HALF * h, HALF * (h + 1))
+            nc.vector.tensor_tensor(out=z_rf[:, cols], in0=late_sums[:, cols], in1=z_early[:, cols], op=ALU.add)
+            nc.scalar.activation(out=act_rf[:, cols], in_=z_rf[:, cols], func=ACT.Sigmoid, scale=-1.0)
+            nc.scalar.activation(out=act_rf[:, cols], in_=act_rf[:, cols], func=ACT.Ln, bias=ln_floor[:, 0:1])
+            if h == 0:
+                nc.scalar.activation(out=steer[:, 1:2], in_=steer[:, 0:1], func=ACT.Sigmoid)
+            nc.scalar.activation(out=act_rf[:, cols], in_=act_rf[:, cols], func=ACT.Tanh, scale=-1.0)
+
+        def rf_product(h):
+            cols = slice(HALF * h, HALF * (h + 1))
+            nc.vector.tensor_tensor(out=rf[:, cols], in0=z_rf[:, cols], in1=act_rf[:, cols], op=ALU.mult)
+
+        def bring_back(h, u):
+            back = psum.tile([P, UNIT, HALF], F32, name="bank")
+            for j in range(UNIT):
+                c, a = divmod(UNIT * u + j, CHUNK)
+                for t in range(2):
+                    nc.tensor.transpose(
+                        back[:, j, P * t : P * (t + 1)], act[c][:, 2 * h + t, P * a : P * (a + 1)], ident[:]
+                    )
+            return back
+
+        def finish(h, u, back):
+            cols = slice(HALF * h, HALF * (h + 1))
+            out_sb = outs.tile([P, UNIT, HALF], F32, name="out_sb")
             nc.vector.tensor_tensor(
-                out=z[u][:],
-                in0=z[u][:],
-                in1=rf[:].unsqueeze(1).to_broadcast([P, UNIT, N_OUT]),
-                op=ALU.add,
+                out=out_sb[:], in0=back[:], in1=rf[:, cols].unsqueeze(1).to_broadcast([P, UNIT, HALF]), op=ALU.add
             )
-            nc.sync.dma_start(out=out[:, UNIT * u : UNIT * (u + 1), :], in_=z[u][:])
+            nc.sync.dma_start(out=out[:, UNIT * u : UNIT * (u + 1), cols], in_=out_sb[:])
+
+        rf_mish(0)
+        staged = {}
+        for q in range(BB_CHUNKS):
+            bb_mish(products[BB_CHUNKS + q])
+            for s in range(LATE + LATE_LOAD * q, LATE + LATE_LOAD * (q + 1)):
+                rf_multiply(s, late_sums, 1, early_last + 1, RF_PASSES - 1)
+            if q < STAGED:
+                staged[q] = bring_back(0, q)
+        rf_mish(1)
+        rf_product(0)
+        for u in range(BB_UNITS):
+            finish(0, u, staged[u] if u in staged else bring_back(0, u))
+        rf_product(1)
+        for u in range(BB_UNITS):
+            finish(1, u, bring_back(1, u))

@@ -30,8 +30,8 @@ RF_AHEAD = 2
 HALF = N_OUT // 2
 LATE = BB_UNITS + 8
 LATE_LOAD = 2
-FIRST_PRODUCT = BB_UNITS + 11
-STAGED = 4
+RF_RUN = 2
+FIRST_PRODUCT = 5
 LN_FLOOR = 2.0 ** -60
 
 FLOPS = 2 * P * K_PASS * N_OUT * (BB_PASSES + RF_PASSES)
@@ -260,27 +260,31 @@ def tile_gnn_layer_pb_k_kernel(
 
         grouped_of = {}
         operand_of = {}
+        steps = [list(range(s, s + RF_RUN)) for s in range(BB_UNITS, UNITS, RF_RUN)]
 
-        def rf_front(s):
-            xt = transpose_unit(s)
-            grouped = stage.tile([P, UNIT, P, 4], BF16, name="grouped", align_bytes=64)
-            copy_unit(xt, grouped[:].bitcast(F32))
-            grouped_of[s] = grouped
+        def rf_front(t):
+            units = steps[t]
+            banks = [transpose_unit(s) for s in units]
+            grouped = stage.tile([P, UNIT * RF_RUN, P, 4], BF16, name="grouped", align_bytes=64)
+            for j in range(RF_RUN):
+                copy_unit(banks[j], grouped[:, UNIT * j : UNIT * (j + 1), :, :].bitcast(F32))
+            grouped_of[t] = grouped
 
-        def rf_quantise(s):
-            if s < LATE:
-                codes = stage.tile([P, UNIT * P], U32, name="codes", align_bytes=64)
-                scales = stage.tile([P, UNIT * P], U8, name="scales", align_bytes=64)
+        def rf_quantise(t):
+            if steps[t][0] < LATE:
+                codes = stage.tile([P, UNIT * RF_RUN * P], U32, name="codes", align_bytes=64)
+                scales = stage.tile([P, UNIT * RF_RUN * P], U8, name="scales", align_bytes=64)
             else:
-                codes = keep.tile([P, UNIT * P], U32, name="late_codes%d" % s, align_bytes=64)
-                scales = keep.tile([P, UNIT * P], U8, name="late_scales%d" % s, align_bytes=64)
-            quantise(grouped_of[s], codes, scales)
-            operand_of[s] = (codes, scales)
+                codes = keep.tile([P, UNIT * RF_RUN * P], U32, name="late_codes%d" % t, align_bytes=64)
+                scales = keep.tile([P, UNIT * RF_RUN * P], U8, name="late_scales%d" % t, align_bytes=64)
+            quantise(grouped_of[t], codes, scales)
+            for j, s in enumerate(steps[t]):
+                operand_of[s] = (codes, scales, UNIT * j)
 
         def rf_multiply(s, sums, columns_h, first, last):
-            codes, scales = operand_of[s]
+            codes, scales, first_block = operand_of[s]
             for a in range(UNIT):
-                rows = slice(P * a, P * (a + 1))
+                rows = slice(P * (first_block + a), P * (first_block + a + 1))
                 g = UNIT * (s - BB_UNITS) + a
                 plane = wrf_planes[g // (2 * PLANE_COLS)]
                 offset = 4 * (g // PLANE_COLS % 2)
@@ -307,22 +311,24 @@ def tile_gnn_layer_pb_k_kernel(
         early_last = UNIT * (LATE - BB_UNITS) - 1
         z_early = keep.tile([P, N_OUT], F32, name="z_early")
         sums_of = {}
-        for s in range(BB_UNITS, UNITS + 2):
-            if s < UNITS:
-                rf_front(s)
-            if BB_UNITS + 1 <= s < UNITS + 1:
-                rf_quantise(s - 1)
-            if BB_UNITS + 2 <= s:
-                if s - 2 == BB_UNITS or s - 2 == LATE:
-                    sums_of[s - 2 >= LATE] = psum_acc.tile([P, N_OUT], F32, name="acc")
-                if s - 2 < LATE:
-                    rf_multiply(s - 2, sums_of[False], None, 0, early_last)
-                else:
-                    rf_multiply(s - 2, sums_of[True], 0, early_last + 1, RF_PASSES - 1)
-                if s - 2 == LATE - 1:
-                    nc.vector.tensor_tensor(out=z_early[:], in0=sums_of[False][:], in1=bias_rf[:], op=ALU.add)
-            if FIRST_PRODUCT <= s - 2 < FIRST_PRODUCT + BB_CHUNKS:
-                bb_mish(products[s - 2 - FIRST_PRODUCT])
+        for t in range(len(steps) + 2):
+            if t < len(steps):
+                rf_front(t)
+            if 1 <= t < len(steps) + 1:
+                rf_quantise(t - 1)
+            if 2 <= t:
+                for s in steps[t - 2]:
+                    if s == BB_UNITS or s == LATE:
+                        sums_of[s >= LATE] = psum_acc.tile([P, N_OUT], F32, name="acc")
+                    if s < LATE:
+                        rf_multiply(s, sums_of[False], None, 0, early_last)
+                    else:
+                        rf_multiply(s, sums_of[True], 0, early_last + 1, RF_PASSES - 1)
+                    if s == LATE - 1:
+                        nc.vector.tensor_tensor(out=z_early[:], in0=sums_of[False][:], in1=bias_rf[:], op=ALU.add)
+                if 0 <= t - 2 - FIRST_PRODUCT < BB_CHUNKS // 2:
+                    for pair in products[2 * (t - 2 - FIRST_PRODUCT) : 2 * (t - 2 - FIRST_PRODUCT) + 2]:
+                        bb_mish(pair)
         late_sums = sums_of[True]
 
         z_rf = keep.tile([P, N_OUT], F32, name="z_rf")
@@ -361,17 +367,14 @@ def tile_gnn_layer_pb_k_kernel(
             nc.sync.dma_start(out=out[:, UNIT * u : UNIT * (u + 1), cols], in_=out_sb[:])
 
         rf_mish(0)
-        staged = {}
         for q in range(BB_CHUNKS):
             bb_mish(products[BB_CHUNKS + q])
             for s in range(LATE + LATE_LOAD * q, LATE + LATE_LOAD * (q + 1)):
                 rf_multiply(s, late_sums, 1, early_last + 1, RF_PASSES - 1)
-            if q < STAGED:
-                staged[q] = bring_back(0, q)
         rf_mish(1)
         rf_product(0)
         for u in range(BB_UNITS):
-            finish(0, u, staged[u] if u in staged else bring_back(0, u))
+            finish(0, u, bring_back(0, u))
         rf_product(1)
         for u in range(BB_UNITS):
             finish(1, u, bring_back(1, u))

@@ -26,7 +26,8 @@ CHUNK = 4
 BB_CHUNKS = BB_PASSES // CHUNK
 PLANE_COLS = 8
 RF_LOAD = 4
-RF_AHEAD = 2
+LAG = 4
+RF_AHEAD = 2 * LAG
 HALF = N_OUT // 2
 LATE = BB_UNITS + 8
 LATE_LOAD = 2
@@ -151,12 +152,10 @@ def tile_gnn_layer_pb_k_kernel(
             load_features(first_unit, 2)
 
         for s in range(BB_UNITS, UNITS):
-            if s == BB_UNITS:
-                load_features(s, RF_LOAD)
-                load_scales(2)
-            if (s - BB_UNITS) % RF_LOAD == RF_LOAD - RF_AHEAD and s + RF_AHEAD < UNITS:
-                load_features(s + RF_AHEAD, RF_LOAD)
-                load_scales(2)
+            for first_unit in range(BB_UNITS, UNITS, RF_LOAD):
+                if first_unit not in features_of and first_unit <= s + RF_AHEAD:
+                    load_features(first_unit, RF_LOAD)
+                    load_scales(2)
             if s < LATE:
                 load_words(s)
             elif (s - LATE) % LATE_LOAD == 0:
@@ -271,12 +270,8 @@ def tile_gnn_layer_pb_k_kernel(
             grouped_of[t] = grouped
 
         def rf_quantise(t):
-            if steps[t][0] < LATE:
-                codes = stage.tile([P, UNIT * RF_RUN * P], U32, name="codes", align_bytes=64)
-                scales = stage.tile([P, UNIT * RF_RUN * P], U8, name="scales", align_bytes=64)
-            else:
-                codes = keep.tile([P, UNIT * RF_RUN * P], U32, name="late_codes%d" % t, align_bytes=64)
-                scales = keep.tile([P, UNIT * RF_RUN * P], U8, name="late_scales%d" % t, align_bytes=64)
+            codes = keep.tile([P, UNIT * RF_RUN * P], U32, name="rf_codes%d" % t, align_bytes=64)
+            scales = keep.tile([P, UNIT * RF_RUN * P], U8, name="rf_scales%d" % t, align_bytes=64)
             quantise(grouped_of[t], codes, scales)
             for j, s in enumerate(steps[t]):
                 operand_of[s] = (codes, scales, UNIT * j)
@@ -311,13 +306,13 @@ def tile_gnn_layer_pb_k_kernel(
         early_last = UNIT * (LATE - BB_UNITS) - 1
         z_early = keep.tile([P, N_OUT], F32, name="z_early")
         sums_of = {}
-        for t in range(len(steps) + 2):
+        for t in range(len(steps) + LAG):
             if t < len(steps):
                 rf_front(t)
             if 1 <= t < len(steps) + 1:
                 rf_quantise(t - 1)
-            if 2 <= t:
-                for s in steps[t - 2]:
+            if LAG <= t:
+                for s in steps[t - LAG]:
                     if s == BB_UNITS or s == LATE:
                         sums_of[s >= LATE] = psum_acc.tile([P, N_OUT], F32, name="acc")
                     if s < LATE:
@@ -326,8 +321,8 @@ def tile_gnn_layer_pb_k_kernel(
                         rf_multiply(s, sums_of[True], 0, early_last + 1, RF_PASSES - 1)
                     if s == LATE - 1:
                         nc.vector.tensor_tensor(out=z_early[:], in0=sums_of[False][:], in1=bias_rf[:], op=ALU.add)
-                if 0 <= t - 2 - FIRST_PRODUCT < BB_CHUNKS // 2:
-                    for pair in products[2 * (t - 2 - FIRST_PRODUCT) : 2 * (t - 2 - FIRST_PRODUCT) + 2]:
+                if 0 <= t - LAG - FIRST_PRODUCT < BB_CHUNKS // 2:
+                    for pair in products[2 * (t - LAG - FIRST_PRODUCT) : 2 * (t - LAG - FIRST_PRODUCT) + 2]:
                         bb_mish(pair)
         late_sums = sums_of[True]
 

@@ -33,6 +33,7 @@ LATE = BB_UNITS + 8
 LATE_LOAD = 2
 RF_RUN = 2
 FIRST_PRODUCT = 5
+HELPED = 3
 LN_FLOOR = 2.0 ** -60
 
 FLOPS = 2 * P * K_PASS * N_OUT * (BB_PASSES + RF_PASSES)
@@ -371,5 +372,17 @@ def tile_gnn_layer_pb_k_kernel(
         for u in range(BB_UNITS):
             finish(0, u, bring_back(0, u))
         rf_product(1)
-        for u in range(BB_UNITS):
+        cols = slice(HALF, N_OUT)
+        helped = []
+        for u in range(BB_UNITS - HELPED, BB_UNITS):
+            back = bring_back(1, u)
+            out_sb = outs.tile([P, UNIT, HALF], F32, name="helped_sb")
+            nc.scalar.copy(out=out_sb[:], in_=back[:])
+            helped.append((u, out_sb))
+        for u, out_sb in helped:
+            nc.gpsimd.tensor_tensor(
+                out=out_sb[:], in0=out_sb[:], in1=rf[:, cols].unsqueeze(1).to_broadcast([P, UNIT, HALF]), op=ALU.add
+            )
+            nc.scalar.dma_start(out=out[:, UNIT * u : UNIT * (u + 1), cols], in_=out_sb[:])
+        for u in range(BB_UNITS - HELPED):
             finish(1, u, bring_back(1, u))

from contextlib import ExitStack

import concourse.mybir as mybir
from concourse.masks import make_identity

F32 = mybir.dt.float32
BF16 = mybir.dt.bfloat16
I32 = mybir.dt.int32
U32 = mybir.dt.uint32
U8 = mybir.dt.uint8
FP8X4 = mybir.dt.float8_e4m3fn_x4
ACT = mybir.ActivationFunctionType
ALU = mybir.AluOpType

P = 128
N_OUT = 512
N_TILES = N_OUT // P
K_PASS = 512
PAIRS_PASS = K_PASS // 2
BB_PASSES = 16
RF_PASSES = 32
UNIT = 2
BB_UNITS = BB_PASSES // UNIT
UNITS = (BB_PASSES + RF_PASSES) // UNIT
CHUNK = 4
BB_CHUNKS = BB_PASSES // CHUNK
PLANE_COLS = 8
RF_LOAD = 4
LAG = 4
RF_AHEAD = 2 * LAG
HALF = N_OUT // 2
LATE = BB_UNITS + 8
LATE_LOAD = 2
RF_RUN = 2
FIRST_PRODUCT = 5
HELPED = 3
LN_FLOOR = 2.0 ** -60

FLOPS = 2 * P * K_PASS * N_OUT * (BB_PASSES + RF_PASSES)


def tile_gnn_layer_pb_k_kernel(
    tc,
    BB_feature,
    RF_feature,
    W_bbbb_words,
    W_bbbb_scales,
    b_bbbb,
    W_rfbb_words,
    W_rfbb_scales,
    b_rfbb,
    out,
):
    nc = tc.nc
    with ExitStack() as stack:
        stack.enter_context(tc.manual_schedule())
        keep = stack.enter_context(tc.tile_pool(name="keep", bufs=1))
        stage = stack.enter_context(tc.tile_pool(name="stage", bufs=3))
        stage_bb = stack.enter_context(tc.tile_pool(name="stage_bb", bufs=2))
        outs = stack.enter_context(tc.tile_pool(name="outs", bufs=4))
        psum = stack.enter_context(tc.psum_pool(name="psum", bufs=7))
        psum_acc = stack.enter_context(tc.psum_pool(name="psum_acc", bufs=1))

        bias_tiles = keep.tile([P, P], BF16, name="bias_tiles")
        nc.vector.memset(bias_tiles[:], 0.0)
        bias_row = keep.tile([P, N_OUT], BF16, name="bias_row")
        nc.vector.memset(bias_row[:], 0.0)
        steer = keep.tile([P, 2], F32, name="steer")
        nc.vector.memset(steer[:], 0.0)
        wbb_plane = keep.tile([P, N_OUT], U8, name="wbb_plane", align_bytes=64)
        nc.vector.memset(wbb_plane[:].bitcast(I32), 0)
        wrf_planes = []
        for half in range(2):
            planes = keep.tile([P, PLANE_COLS, N_OUT], U8, name="wrf_planes%d" % half, align_bytes=64)
            nc.vector.memset(planes[:].bitcast(I32), 0)
            wrf_planes.append(planes)
        ones = keep.tile([P, P], BF16, name="ones")
        nc.vector.memset(ones[:], 1.0)
        ln_floor = keep.tile([P, 1], F32, name="ln_floor")
        nc.vector.memset(ln_floor[:], LN_FLOOR)
        ident = keep.tile([P, P], F32, name="ident")
        make_identity(nc, ident[:])
        ident_bf = keep.tile([P, P], BF16, name="ident_bf")
        make_identity(nc, ident_bf[:])

        features_of = {}

        def load_features(first_unit, units):
            passes = UNIT * units
            rows_sb = keep.tile([P, passes * K_PASS], BF16, name="features%d" % first_unit)
            if first_unit < BB_UNITS:
                g = UNIT * first_unit
                rows = BB_feature[:, g : g + passes, :].rearrange("b g k -> b (g k)")
            else:
                first = UNIT * (first_unit - BB_UNITS) * K_PASS
                rows = RF_feature[:, first : first + passes * K_PASS]
            nc.sync.dma_start(out=rows_sb[:], in_=rows)
            for j in range(units):
                features_of[first_unit + j] = (rows_sb, UNIT * j)

        def packed_words(dram_words):
            return dram_words.rearrange("g p n t -> p g (n t)").bitcast(I32)

        wrf_words = {}

        def load_words(s):
            g = UNIT * (s - BB_UNITS)
            words = keep.tile([P, UNIT, N_OUT], U32, name="wrf_words%d" % s, align_bytes=64)
            nc.sync.dma_start(out=words[:].bitcast(I32), in_=packed_words(W_rfbb_words[g : g + UNIT]))
            wrf_words[s] = words

        half_words = {}

        def load_half_words(s, h):
            g = UNIT * (s - BB_UNITS)
            passes = UNIT * LATE_LOAD
            words = keep.tile([P, passes, HALF], U32, name="half_words%d_%d" % (s, h), align_bytes=64)
            nc.sync.dma_start(
                out=words[:].bitcast(I32),
                in_=packed_words(W_rfbb_words[g : g + passes, :, HALF * h : HALF * (h + 1), :]),
            )
            for j in range(LATE_LOAD):
                half_words[(s + j, h)] = (words, UNIT * j)

        scale_loads = [(half, share, r) for half in range(2) for share in range(2) for r in range(4)]

        def load_scales(count):
            for load in scale_loads[:count]:
                half, share, r = load
                first = 2 * PLANE_COLS * half + PLANE_COLS * share
                nc.sync.dma_start(
                    out=wrf_planes[half][4 * share + r : P : 32, :, :].bitcast(I32),
                    in_=W_rfbb_scales[first : first + PLANE_COLS, r : 16 : 4, :]
                    .rearrange("j q n -> q j n")
                    .bitcast(I32),
                )
                scale_loads.remove(load)

        nc.scalar.dma_start(out=bias_tiles[0:N_TILES, :], in_=b_bbbb.rearrange("(i m) -> i m", i=N_TILES))
        nc.scalar.dma_start(out=bias_row[0:1, :], in_=b_rfbb.rearrange("(o n) -> o n", o=1))
        nc.scalar.activation(out=steer[:, 1:2], in_=steer[:, 0:1], func=ACT.Sigmoid)

        load_features(0, 1)
        wbb_words = keep.tile([P, 1, N_OUT], U32, name="wbb_words", align_bytes=64)
        nc.sync.dma_start(out=wbb_words[:].bitcast(I32), in_=packed_words(W_bbbb_words))
        for r in range(4):
            nc.sync.dma_start(
                out=wbb_plane[r : P : 32, :].bitcast(I32),
                in_=W_bbbb_scales[0, r : 16 : 4, :].bitcast(I32),
            )
        load_features(1, 1)
        for first_unit in range(2, BB_UNITS, 2):
            load_features(first_unit, 2)

        for s in range(BB_UNITS, UNITS):
            for first_unit in range(BB_UNITS, UNITS, RF_LOAD):
                if first_unit not in features_of and first_unit <= s + RF_AHEAD:
                    load_features(first_unit, RF_LOAD)
                    load_scales(2)
            if s < LATE:
                load_words(s)
            elif (s - LATE) % LATE_LOAD == 0:
                load_half_words(s, 0)
            load_scales(2)
        for s in range(LATE, UNITS, LATE_LOAD):
            load_half_words(s, 1)

        columns = psum.tile([P, N_OUT], F32, name="bank")
        nc.tensor.matmul(
            out=columns[:, 0:N_TILES], lhsT=bias_tiles[:], rhs=ident_bf[:, 0:N_TILES], start=True, stop=True
        )
        bias_bb = keep.tile([P, N_TILES], F32, name="bias_bb")
        nc.vector.tensor_copy(out=bias_bb[:], in_=columns[:, 0:N_TILES])
        minus_bias_bb = keep.tile([P, N_TILES], F32, name="minus_bias_bb")
        nc.vector.tensor_scalar_mul(out=minus_bias_bb[:], in0=columns[:, 0:N_TILES], scalar1=-1.0)
        spread = psum.tile([P, N_OUT], F32, name="bank")
        nc.tensor.matmul(out=spread[:], lhsT=ones[:], rhs=bias_row[:], start=True, stop=True)
        bias_rf = keep.tile([P, N_OUT], F32, name="bias_rf")
        nc.vector.tensor_copy(out=bias_rf[:], in_=spread[:])

        def transpose_unit(s):
            rows_sb, first_pass = features_of[s]
            pairs = rows_sb[:].bitcast(F32)
            xt = psum.tile([P, UNIT, 2, P], F32, name="bank")
            for a in range(UNIT):
                first = (first_pass + a) * PAIRS_PASS
                for u in range(2):
                    nc.tensor.transpose(
                        xt[:, a, u, :], pairs[:, first + u : first + PAIRS_PASS : 2], ident[:]
                    )
            return xt

        def copy_unit(xt, words):
            nc.vector.tensor_copy(out=words, in_=xt[:].rearrange("p a u b -> p a b u"))

        def quantise(grouped, codes, scales):
            nc.vector.quantize_mx(
                out=codes[:].bitcast(FP8X4), scales=scales[:], in_=grouped[:].rearrange("p a b t -> p (a b t)")
            )

        bb_codes = [keep.tile([P, CHUNK * P], U32, name="bb_codes%d" % c, align_bytes=64) for c in range(BB_CHUNKS)]
        bb_scales = [keep.tile([P, CHUNK * P], U8, name="bb_scales%d" % c, align_bytes=64) for c in range(BB_CHUNKS)]
        act = [keep.tile([P, N_TILES, N_OUT], F32, name="act%d" % c) for c in range(BB_CHUNKS)]

        def bb_product(c, i):
            features_i = slice(P * i, P * (i + 1))
            zt = psum.tile([P, N_OUT], F32, name="bank")
            nc.tensor.matmul_mx(
                out=zt[:],
                lhsT=wbb_words[:, 0, features_i].bitcast(FP8X4),
                lhsT_scale=wbb_plane[:, features_i],
                rhs=bb_codes[c][:].bitcast(FP8X4),
                rhs_scale=bb_scales[c][:],
                start=True,
                stop=True,
            )
            return zt

        def bb_front(c):
            banks = [transpose_unit(2 * c + j) for j in range(2)]
            grouped = stage_bb.tile([P, CHUNK, P, 4], BF16, name="grouped_bb", align_bytes=64)
            for j in range(2):
                copy_unit(banks[j], grouped[:, UNIT * j : UNIT * (j + 1), :, :].bitcast(F32))
            quantise(grouped, bb_codes[c], bb_scales[c])

        def bb_sigmoids(c):
            for i in range(N_TILES):
                zt = bb_product(c, i)
                nc.scalar.activation(
                    out=act[c][:, i, :], in_=zt[:], func=ACT.Sigmoid, scale=-1.0, bias=minus_bias_bb[:, i : i + 1]
                )

        bb_front(0)
        for c in range(BB_CHUNKS):
            if c + 1 < BB_CHUNKS:
                bb_front(c + 1)
            bb_sigmoids(c)

        for c in range(BB_CHUNKS):
            nc.scalar.activation(out=act[c][:], in_=act[c][:], func=ACT.Ln, bias=ln_floor[:, 0:1])
        nc.scalar.activation(out=steer[:, 1:2], in_=steer[:, 0:1], func=ACT.Sigmoid)
        products = []
        for h in range(2):
            for c in range(BB_CHUNKS):
                pair = act[c][:, 2 * h : 2 * h + 2, :]
                nc.scalar.activation(out=pair, in_=pair, func=ACT.Tanh, scale=-1.0)
                products.append([(c, 2 * h), (c, 2 * h + 1)])

        def bb_mish(pair):
            for c, i in pair:
                zt = bb_product(c, i)
                nc.vector.scalar_tensor_tensor(
                    out=act[c][:, i, :],
                    in0=zt[:],
                    scalar=bias_bb[:, i : i + 1],
                    in1=act[c][:, i, :],
                    op0=ALU.add,
                    op1=ALU.mult,
                )

        grouped_of = {}
        operand_of = {}
        steps = [list(range(s, s + RF_RUN)) for s in range(BB_UNITS, UNITS, RF_RUN)]

        def rf_front(t):
            units = steps[t]
            banks = [transpose_unit(s) for s in units]
            grouped = stage.tile([P, UNIT * RF_RUN, P, 4], BF16, name="grouped", align_bytes=64)
            for j in range(RF_RUN):
                copy_unit(banks[j], grouped[:, UNIT * j : UNIT * (j + 1), :, :].bitcast(F32))
            grouped_of[t] = grouped

        def rf_quantise(t):
            codes = keep.tile([P, UNIT * RF_RUN * P], U32, name="rf_codes%d" % t, align_bytes=64)
            scales = keep.tile([P, UNIT * RF_RUN * P], U8, name="rf_scales%d" % t, align_bytes=64)
            quantise(grouped_of[t], codes, scales)
            for j, s in enumerate(steps[t]):
                operand_of[s] = (codes, scales, UNIT * j)

        def rf_multiply(s, sums, columns_h, first, last):
            codes, scales, first_block = operand_of[s]
            for a in range(UNIT):
                rows = slice(P * (first_block + a), P * (first_block + a + 1))
                g = UNIT * (s - BB_UNITS) + a
                plane = wrf_planes[g // (2 * PLANE_COLS)]
                offset = 4 * (g // PLANE_COLS % 2)
                if columns_h is None:
                    target = sums[:]
                    rhs = wrf_words[s][:, a, :]
                    rhs_scale = plane[offset:P, g % PLANE_COLS, :]
                else:
                    cols = slice(HALF * columns_h, HALF * (columns_h + 1))
                    words, first_pass = half_words[(s, columns_h)]
                    target = sums[:, cols]
                    rhs = words[:, first_pass + a, :]
                    rhs_scale = plane[offset:P, g % PLANE_COLS, cols]
                nc.tensor.matmul_mx(
                    out=target,
                    lhsT=codes[:, rows].bitcast(FP8X4),
                    lhsT_scale=scales[:, rows],
                    rhs=rhs.bitcast(FP8X4),
                    rhs_scale=rhs_scale,
                    start=(g == first),
                    stop=(g == last),
                )

        early_last = UNIT * (LATE - BB_UNITS) - 1
        z_early = keep.tile([P, N_OUT], F32, name="z_early")
        sums_of = {}
        for t in range(len(steps) + LAG):
            if t < len(steps):
                rf_front(t)
            if 1 <= t < len(steps) + 1:
                rf_quantise(t - 1)
            if LAG <= t:
                for s in steps[t - LAG]:
                    if s == BB_UNITS or s == LATE:
                        sums_of[s >= LATE] = psum_acc.tile([P, N_OUT], F32, name="acc")
                    if s < LATE:
                        rf_multiply(s, sums_of[False], None, 0, early_last)
                    else:
                        rf_multiply(s, sums_of[True], 0, early_last + 1, RF_PASSES - 1)
                    if s == LATE - 1:
                        nc.vector.tensor_tensor(out=z_early[:], in0=sums_of[False][:], in1=bias_rf[:], op=ALU.add)
                if 0 <= t - LAG - FIRST_PRODUCT < BB_CHUNKS // 2:
                    for pair in products[2 * (t - LAG - FIRST_PRODUCT) : 2 * (t - LAG - FIRST_PRODUCT) + 2]:
                        bb_mish(pair)
        late_sums = sums_of[True]

        z_rf = keep.tile([P, N_OUT], F32, name="z_rf")
        act_rf = keep.tile([P, N_OUT], F32, name="act_rf")
        rf = keep.tile([P, N_OUT], F32, name="rf")

        def rf_mish(h):
            cols = slice(HALF * h, HALF * (h + 1))
            nc.vector.tensor_tensor(out=z_rf[:, cols], in0=late_sums[:, cols], in1=z_early[:, cols], op=ALU.add)
            nc.scalar.activation(out=act_rf[:, cols], in_=z_rf[:, cols], func=ACT.Sigmoid, scale=-1.0)
            nc.scalar.activation(out=act_rf[:, cols], in_=act_rf[:, cols], func=ACT.Ln, bias=ln_floor[:, 0:1])
            if h == 0:
                nc.scalar.activation(out=steer[:, 1:2], in_=steer[:, 0:1], func=ACT.Sigmoid)
            nc.scalar.activation(out=act_rf[:, cols], in_=act_rf[:, cols], func=ACT.Tanh, scale=-1.0)

        def rf_product(h):
            cols = slice(HALF * h, HALF * (h + 1))
            nc.vector.tensor_tensor(out=rf[:, cols], in0=z_rf[:, cols], in1=act_rf[:, cols], op=ALU.mult)

        def bring_back(h, u):
            back = psum.tile([P, UNIT, HALF], F32, name="bank")
            for j in range(UNIT):
                c, a = divmod(UNIT * u + j, CHUNK)
                for t in range(2):
                    nc.tensor.transpose(
                        back[:, j, P * t : P * (t + 1)], act[c][:, 2 * h + t, P * a : P * (a + 1)], ident[:]
                    )
            return back

        def finish(h, u, back):
            cols = slice(HALF * h, HALF * (h + 1))
            out_sb = outs.tile([P, UNIT, HALF], F32, name="out_sb")
            nc.vector.tensor_tensor(
                out=out_sb[:], in0=back[:], in1=rf[:, cols].unsqueeze(1).to_broadcast([P, UNIT, HALF]), op=ALU.add
            )
            nc.sync.dma_start(out=out[:, UNIT * u : UNIT * (u + 1), cols], in_=out_sb[:])

        rf_mish(0)
        for q in range(BB_CHUNKS):
            bb_mish(products[BB_CHUNKS + q])
            for s in range(LATE + LATE_LOAD * q, LATE + LATE_LOAD * (q + 1)):
                rf_multiply(s, late_sums, 1, early_last + 1, RF_PASSES - 1)
        rf_mish(1)
        rf_product(0)
        for u in range(BB_UNITS):
            finish(0, u, bring_back(0, u))
        rf_product(1)
        cols = slice(HALF, N_OUT)
        helped = []
        for u in range(BB_UNITS - HELPED, BB_UNITS):
            back = bring_back(1, u)
            out_sb = outs.tile([P, UNIT, HALF], F32, name="helped_sb")
            nc.scalar.copy(out=out_sb[:], in_=back[:])
            helped.append((u, out_sb))
        for u, out_sb in helped:
            nc.gpsimd.tensor_tensor(
                out=out_sb[:], in0=out_sb[:], in1=rf[:, cols].unsqueeze(1).to_broadcast([P, UNIT, HALF]), op=ALU.add
            )
            nc.scalar.dma_start(out=out[:, UNIT * u : UNIT * (u + 1), cols], in_=out_sb[:])
        for u in range(BB_UNITS - HELPED):
            finish(1, u, bring_back(1, u))
